import numpy as np
import ml_dtypes


def mxq(x, axis, fmt="e4m3"):
    dtype, down = {"e4m3": (ml_dtypes.float8_e4m3fn, 7), "e5m2": (ml_dtypes.float8_e5m2, 14)}[fmt]
    v = np.moveaxis(np.asarray(x, np.float32).astype(ml_dtypes.bfloat16).astype(np.float64), axis, -1)
    blocks = v.reshape(v.shape[:-1] + (-1, 32))
    amax = np.abs(blocks).max(-1, keepdims=True)
    byte = np.maximum(np.where(amax > 0, np.frexp(amax)[1] - 1 + 127, 0) - down, 1)
    scale = np.exp2(byte - 127.0)
    codes = (blocks / scale).astype(np.float32).astype(dtype).astype(np.float64)
    return np.moveaxis((codes * scale).reshape(v.shape), -1, axis)


WIDE = False


def mx_kscale(k):
    if not WIDE:
        return np.ones(k)
    levels = np.array([10, -10, 5, -5, 0])
    if k % 512:
        return np.exp2(np.random.permutation(np.resize(levels, k // 32))).repeat(32)
    a = np.empty((k // 512, 16))
    for p in range(k // 512):
        a[p, :8] = np.random.permutation(np.resize(levels, 8))
        for g in range(8):
            far = levels[np.abs(levels - a[p, g]) >= 10]
            a[p, g + 8] = far[np.random.randint(len(far))]
    return np.exp2(a.ravel()).repeat(32)


BF16 = ml_dtypes.bfloat16


def bf(x):
    return np.asarray(x, np.float32).astype(BF16)


def f64(x):
    return np.asarray(x).astype(np.float64)


B, H, W, C, NH, WS, SHIFT, F = 8, 32, 32, 2048, 64, 8, 3, 2048
S = WS * WS
HD = C // NH
NWIN = B * (H // WS) * (W // WS)
EPS = 1e-5


def layer_norm(x, w, b):
    m = x.mean(-1, keepdims=True)
    v = ((x - m) ** 2).mean(-1, keepdims=True)
    return (x - m) / np.sqrt(v + EPS) * w + b


def erf(z):
    a = np.clip(z, -6.0, 6.0)
    t2 = 2.0 * a * a
    term = a.copy()
    tot = a.copy()
    for n in range(1, 110):
        term = term * t2 / (2 * n + 1)
        tot = tot + term
    return 2.0 / np.sqrt(np.pi) * np.exp(-a * a) * tot


def gelu(v):
    return 0.5 * v * (1.0 + erf(v / np.sqrt(2.0)))


def setup_inputs():
    s = mx_kscale(C)
    t = mx_kscale(C)
    return {"o_heads": bf(0.25 * np.random.standard_normal((NWIN, NH, S, HD)) * s.reshape(NH, 1, HD)),
            "x": bf(np.random.standard_normal((B, H * W, C))),
            "out_w": bf(2.0 * np.random.standard_normal((C, C)) / np.sqrt(C) / s[None, :]),
            "out_b": bf(0.1 * np.random.standard_normal(C)),
            "norm2_w": bf((1.0 + 0.1 * np.random.standard_normal(C)) * t),
            "norm2_b": bf(0.1 * np.random.standard_normal(C) * t),
            "fc1_w": bf(np.random.standard_normal((F, C)) / np.sqrt(C) / t[None, :]),
            "fc1_b": bf(0.1 * np.random.standard_normal(F))}


def reference(o_heads, x, out_w, out_b, norm2_w, norm2_b, fc1_w, fc1_b):
    o = f64(o_heads).transpose(0, 2, 1, 3).reshape(-1, S, C)
    o = (mxq(o, 2, "e4m3") @ mxq(f64(out_w), 1, "e4m3").T) + f64(out_b)
    o = o.reshape(B, H // WS, W // WS, WS, WS, C)
    o = o.transpose(0, 1, 3, 2, 4, 5).reshape(B, H, W, C)
    o = np.roll(o, (SHIFT, SHIFT), axis=(1, 2))
    x2 = f64(x) + o.reshape(B, H * W, C)
    h2 = layer_norm(x2, f64(norm2_w), f64(norm2_b))
    g = gelu((mxq(h2, 2, "e4m3") @ mxq(f64(fc1_w), 1, "e4m3").T) + f64(fc1_b))
    return x2, g

@@ -1,0 +1,390 @@
+from contextlib import ExitStack
+
+import concourse.mybir as mybir
+from concourse.masks import make_identity
+
+FLOPS = 2 * 2 * 8192 * 2048 * 2048
+
+F32 = mybir.dt.float32
+BF16 = mybir.dt.bfloat16
+U32 = mybir.dt.uint32
+U8 = mybir.dt.uint8
+FP8X4 = mybir.dt.float8_e4m3fn_x4
+ALU = mybir.AluOpType
+ACT = mybir.ActivationFunctionType
+AX = mybir.AxisListType
+
+P = 128
+C = 2048
+NT = 64
+EPS = 1e-5
+
+
+def rotation_segments(shift):
+    if shift == 0:
+        return [(0, 4, 0, 4)]
+    return [(1, 4, 0, 3), (0, 1, 3, 4)]
+
+
+def tile_swintransformerblock_pb_l_kernel(
+    tc, o_heads, x, out_w, out_b, norm2_w, norm2_b, fc1_w, fc1_b, out_0, out_1
+):
+    nc = tc.nc
+    with ExitStack() as ctx:
+        keep = ctx.enter_context(tc.tile_pool(name="keep", bufs=1))
+        work = ctx.enter_context(tc.tile_pool(name="work", bufs=2))
+        psum = ctx.enter_context(tc.psum_pool(name="psum", bufs=8))
+        ctx.enter_context(tc.manual_schedule())
+
+        grid = "b (iw ri jw cj) ch -> (b iw) ri jw cj ch"
+        x_v = x.rearrange(grid, iw=4, ri=8, jw=4, cj=8)
+        x2_v = out_0.rearrange(grid, iw=4, ri=8, jw=4, cj=8)
+        g_v = out_1.rearrange(grid, iw=4, ri=8, jw=4, cj=8)
+        oh_v = o_heads.rearrange("n a s d -> n a (s d)")
+
+        warm = keep.tile([P, 1], F32, name="warm")
+        nc.vector.memset(warm[:], 0.0)
+        nc.scalar.activation(out=warm[:], in_=warm[:], func=ACT.Gelu)
+        mhalf = keep.tile([P, 1], F32, name="mhalf")
+        nc.vector.memset(mhalf[:], -0.5)
+
+        ident = keep.tile([P, P], F32, name="ident")
+        make_identity(nc, ident[:])
+        ident_v = ident.rearrange("n (b i j) -> n b i j", b=8, i=4, j=4)
+        perm = {(0, 0): ident}
+        for dr, dc in ((0, 1), (1, 0), (1, 1)):
+            pm = keep.tile([P, P], F32, name="perm%d%d" % (dr, dc))
+            pm_v = pm.rearrange("n (b i j) -> n b i j", b=8, i=4, j=4)
+            for i0, i1, s0, s1 in rotation_segments(dr):
+                for j0, j1, t0, t1 in rotation_segments(dc):
+                    nc.vector.tensor_copy(out=pm_v[:, :, i0:i1, j0:j1], in_=ident_v[:, :, s0:s1, t0:t1])
+            perm[(dr, dc)] = pm
+
+        w1c = keep.tile([P, 4, C], U32, name="w1c", align_bytes=64)
+        w1s = keep.tile([P, 4, C], U8, name="w1s", align_bytes=64)
+        w2c = keep.tile([P, 4, C], U32, name="w2c", align_bytes=64)
+        w2s = keep.tile([P, 4, C], U8, name="w2s", align_bytes=64)
+        ob = keep.tile([P, C], BF16, name="ob")
+        fb = keep.tile([P, C], BF16, name="fb")
+        wraw = keep.tile([P, 16], BF16, name="wraw")
+        braw = keep.tile([P, 16], BF16, name="braw")
+        wcol = keep.tile([P, 16], F32, name="wcol")
+        bcol = keep.tile([P, 16], F32, name="bcol")
+
+        rows = {}
+
+        def load_rows(w, key, part):
+            wr = work.tile([P, 2 * C], BF16, tag=("zs" if part % 2 == 0 else "go"))
+            w_v = w.rearrange("(l r p) k -> l p r k", l=8, r=2, p=P)
+            nc.sync.dma_start(out=wr.rearrange("p (r k) -> p r k", r=2), in_=w_v[part])
+            rows[(key, part)] = wr
+
+        def prep_rows(key, part, wc, ws):
+            ww = rows[(key, part)].bitcast(F32)
+            cols = slice(256 * part, 256 * (part + 1))
+            for g in range(4):
+                pt = psum.tile([P, 4, P], F32, tag="ps")
+                for r in range(2):
+                    for u in range(2):
+                        base = 1024 * r + 256 * g
+                        nc.tensor.transpose(pt[:, 2 * r + u, :], ww[:, base + u : base + 256 : 2], ident[:])
+                gw = work.tile([P, C], BF16, tag="gm", align_bytes=64)
+                dst = gw[:, 0:1024].bitcast(F32).rearrange("p (r c u) -> p r c u", r=2, c=P, u=2)
+                src = pt.rearrange("p (r u) c -> p r c u", r=2, u=2)
+                if g % 2 == 0:
+                    nc.vector.tensor_copy(out=dst, in_=src)
+                else:
+                    nc.scalar.copy(out=dst, in_=src)
+                rows[(key, part, g)] = gw
+                if g >= 1:
+                    nc.vector.quantize_mx(
+                        out=wc[:, g - 1, cols].bitcast(FP8X4), scales=ws[:, g - 1, cols],
+                        in_=rows[(key, part, g - 1)][:, 0:1024],
+                    )
+            nc.vector.quantize_mx(out=wc[:, 3, cols].bitcast(FP8X4), scales=ws[:, 3, cols], in_=rows[(key, part, 3)][:, 0:1024])
+
+        staged = {}
+        x_in = {}
+        x_sum = {}
+        sorted_m = {}
+        m_grp = {}
+        m_q = {}
+        stat = {}
+        z_srt = {}
+        h_t = {}
+        h_grp = {}
+        h_q = {}
+        g_out = {}
+
+        def ok(i):
+            return 0 <= i < NT
+
+        def place(i):
+            return (i // 8 + 3) % 8, (i % 8 + 3) % 8
+
+        def load_stage(grp, q):
+            if q == 0:
+                st = work.tile([P, 4 * C], BF16, tag="st")
+                staged[grp] = st
+            st_v = staged[grp].rearrange("p (a e) -> p a e", a=64)
+            off = 128 * grp
+            heads = slice(16 * q, 16 * (q + 1))
+            nc.sync.dma_start(out=st_v[:, heads, :], in_=oh_v[:, heads, off : off + 128])
+
+        def load_x(i):
+            ri, cj = place(i)
+            xt = work.tile([P, C], BF16, tag="xt", bufs=3)
+            for jw in range(4):
+                nc.sync.dma_start(out=xt[jw:P:4, :], in_=x_v[:, ri, jw, cj, :])
+            x_in[i] = xt
+
+        def store_x2(i):
+            ri, cj = place(i)
+            for jw in range(4):
+                nc.sync.dma_start(out=x2_v[:, ri, jw, cj, :], in_=x_sum[i][jw:P:4, :])
+
+        def store_g(i):
+            ri, cj = place(i)
+            for jw in range(4):
+                nc.sync.dma_start(out=g_v[:, ri, jw, cj, :], in_=g_out[i][jw:P:4, :])
+
+        def add_bias(i, j):
+            if j == 0:
+                xb = work.tile([P, C], F32, tag="xb", bufs=3)
+                x_sum[i] = xb
+            for cols in (slice(512 * j, 512 * j + 256), slice(512 * j + 256, 512 * j + 512)):
+                nc.gpsimd.tensor_tensor(out=x_sum[i][:, cols], in0=x_in[i][:, cols], in1=ob[:, cols], op=ALU.add)
+
+        def sort_m(i, u):
+            if u == 0:
+                srt = work.tile([P, 1024], F32, tag="srt")
+                sorted_m[i] = srt
+            st_w = staged[i // 4].bitcast(F32).rearrange("p (a c dh u) -> p a c dh u", a=64, c=4, dh=8, u=2)
+            nc.vector.tensor_copy(
+                out=sorted_m[i].rearrange("p (u a dh) -> p u a dh", u=2, a=64, dh=8)[:, u],
+                in_=st_w[:, :, i % 4, :, u],
+            )
+
+        def turn_m(i):
+            srt = sorted_m[i]
+            pm = perm[((i // 8 + 3) // 8, (i % 8 + 3) // 8)]
+            gm = work.tile([P, C], BF16, tag="gm", align_bytes=64)
+            gm_v = gm.bitcast(F32).rearrange("p (j gg q u) -> p j gg q u", j=2, gg=2, q=P, u=2)
+            for j in range(2):
+                pt = psum.tile([P, 4, P], F32, tag="ps")
+                for gg in range(2):
+                    for u in range(2):
+                        col = 512 * u + 128 * (2 * j + gg)
+                        nc.tensor.transpose(pt[:, 2 * gg + u, :], srt[:, col : col + 128], pm[:])
+                nc.scalar.copy(out=gm_v[:, j], in_=pt.rearrange("p (gg u) q -> p gg q u", gg=2, u=2))
+            m_grp[i] = gm
+
+        def quant_m(i):
+            mc = work.tile([P, 512], U32, tag="mc", align_bytes=64)
+            ms = work.tile([P, 512], U8, tag="ms", align_bytes=64)
+            nc.vector.quantize_mx(out=mc.bitcast(FP8X4), scales=ms[:], in_=m_grp[i][:])
+            m_q[i] = (mc, ms)
+
+        def mx_chunk(ps, ac, asc, wc, ws, j):
+            cols = slice(512 * j, 512 * (j + 1))
+            for g in range(4):
+                tok = slice(P * g, P * (g + 1))
+                nc.tensor.matmul_mx(
+                    out=ps[:],
+                    lhsT=ac[:, tok].bitcast(FP8X4),
+                    lhsT_scale=asc[:, tok],
+                    rhs=wc[:, g, cols].bitcast(FP8X4),
+                    rhs_scale=ws[:, g, cols],
+                    start=(g == 0),
+                    stop=(g == 3),
+                )
+
+        def proj(i, j):
+            if j == 0:
+                sums = work.tile([P, 4], F32, tag="sums", bufs=3)
+                stat[(i, "sums")] = sums
+            mc, ms = m_q[i]
+            xb = x_sum[i]
+            cols = slice(512 * j, 512 * (j + 1))
+            ps = psum.tile([P, 512], F32, tag="ps")
+            mx_chunk(ps, mc, ms, w1c, w1s, j)
+            nc.vector.scalar_tensor_tensor(
+                out=xb[:, cols], in0=ps[:], scalar=1.0, in1=xb[:, cols], op0=ALU.mult, op1=ALU.add,
+                accum_out=stat[(i, "sums")][:, j : j + 1],
+            )
+
+        def mean(i):
+            part = work.tile([P, 4], F32, tag="part", bufs=3)
+            negmean = work.tile([P, 1], F32, tag="negmean", bufs=3)
+            nc.vector.tensor_scalar(
+                out=part[:], in0=stat[(i, "sums")][:], scalar1=-1.0 / C, scalar2=None, op0=ALU.mult, op1=ALU.add,
+                accum_out=negmean[:],
+            )
+            stat[(i, "negmean")] = negmean
+
+        def squares(i):
+            zs = work.tile([P, C], F32, tag="zs")
+            ssq = work.tile([P, 1], F32, tag="ssq", bufs=3)
+            nc.scalar.activation(
+                out=zs[:], in_=x_sum[i][:], func=ACT.Square, bias=stat[(i, "negmean")][:], scale=1.0, accum_out=ssq[:]
+            )
+            z_srt[i] = zs
+            stat[(i, "ssq")] = ssq
+
+        def inv_std(i):
+            ve = work.tile([P, 1], F32, tag="ve", bufs=3)
+            nc.gpsimd.tensor_scalar(
+                out=ve[:], in0=stat[(i, "ssq")][:], scalar1=1.0 / C, scalar2=EPS, op0=ALU.mult, op1=ALU.add
+            )
+            rstd = work.tile([P, 1], F32, tag="rstd", bufs=3)
+            nc.gpsimd.tensor_tensor(out=rstd[:], in0=ve[:], in1=mhalf[:], op=ALU.pow)
+            nmr = work.tile([P, 1], F32, tag="nmr", bufs=3)
+            nc.gpsimd.tensor_tensor(out=nmr[:], in0=rstd[:], in1=stat[(i, "negmean")][:], op=ALU.mult)
+            stat[(i, "rstd")] = rstd
+            stat[(i, "nmr")] = nmr
+
+        def normalise(i, engine):
+            z_v = z_srt[i].rearrange("q (g t m) -> q g t m", g=4, t=4, m=P)
+            x_r = x_sum[i].rearrange("q (g m t) -> q g t m", g=4, m=P, t=4)
+            if engine == "vector":
+                nc.vector.tensor_scalar(
+                    out=z_v[:, 0:2], in0=x_r[:, 0:2], scalar1=stat[(i, "negmean")][:], scalar2=stat[(i, "rstd")][:],
+                    op0=ALU.add, op1=ALU.mult,
+                )
+            else:
+                nc.scalar.activation(
+                    out=z_v[:, 2:4], in_=x_r[:, 2:4], func=ACT.Identity, bias=stat[(i, "nmr")][:], scale=stat[(i, "rstd")][:]
+                )
+
+        def turn_h(i, g):
+            if g == 0:
+                ht = work.tile([P, 16, P], BF16, tag="ht")
+                h_t[i] = ht
+            zs = z_srt[i]
+            pt = psum.tile([P, 4, P], F32, tag="ps")
+            for t in range(4):
+                k = 4 * g + t
+                nc.tensor.transpose(pt[:, t, :], zs[:, P * k : P * (k + 1)], ident[:])
+            for t in range(4):
+                k = 4 * g + t
+                nc.scalar.activation(
+                    out=h_t[i][:, k, :], in_=pt[:, t, :], func=ACT.Identity, bias=bcol[:, k : k + 1], scale=wcol[:, k : k + 1]
+                )
+
+        def weave_h(i, half):
+            if half == 0:
+                gh = work.tile([P, C], BF16, tag="gh", align_bytes=64)
+                h_grp[i] = gh
+            nc.vector.tensor_copy(
+                out=h_grp[i].rearrange("p (g q t) -> p g q t", g=4, q=P, t=4)[:, 2 * half : 2 * half + 2],
+                in_=h_t[i].rearrange("p (g t) q -> p g q t", g=4, t=4)[:, 2 * half : 2 * half + 2],
+            )
+
+        def quant_h(i):
+            hc = work.tile([P, 512], U32, tag="hc", align_bytes=64)
+            hs = work.tile([P, 512], U8, tag="hs", align_bytes=64)
+            nc.vector.quantize_mx(out=hc.bitcast(FP8X4), scales=hs[:], in_=h_grp[i][:])
+            h_q[i] = (hc, hs)
+
+        def fc1(i, j):
+            if j == 0:
+                go = work.tile([P, C], F32, tag="go")
+                g_out[i] = go
+            hc, hs = h_q[i]
+            go = g_out[i]
+            cols = slice(512 * j, 512 * (j + 1))
+            ps = psum.tile([P, 512], F32, tag="ps")
+            mx_chunk(ps, hc, hs, w2c, w2s, j)
+            nc.vector.tensor_tensor(out=go[:, cols], in0=ps[:], in1=fb[:, cols], op=ALU.add)
+
+        def gelu(i, j):
+            cols = slice(512 * j, 512 * (j + 1))
+            nc.scalar.activation(out=g_out[i][:, cols], in_=g_out[i][:, cols], func=ACT.Gelu)
+
+        for part in range(4):
+            load_rows(out_w, 1, part)
+        nc.sync.dma_start(out=ob[:], in_=out_b.partition_broadcast(P))
+        for part in range(8):
+            prep_rows(1, part, w1c, w1s)
+            if part + 4 < 8:
+                load_rows(out_w, 1, part + 4)
+            if part == 3:
+                for q in range(4):
+                    load_stage(0, q)
+                load_x(0)
+        nc.sync.dma_start(out=fb[:], in_=fc1_b.partition_broadcast(P))
+        nc.sync.dma_start(
+            out=wraw.rearrange("p (g t) -> p g t", g=4), in_=norm2_w.rearrange("(g p t) -> p g t", g=4, p=P, t=4)
+        )
+        nc.sync.dma_start(
+            out=braw.rearrange("p (g t) -> p g t", g=4), in_=norm2_b.rearrange("(g p t) -> p g t", g=4, p=P, t=4)
+        )
+        nc.vector.tensor_copy(out=wcol[:], in_=wraw[:])
+        nc.vector.tensor_copy(out=bcol[:], in_=braw[:])
+        for part in range(4):
+            load_rows(fc1_w, 2, part)
+
+        for s in range(-4, NT + 2):
+            if ok(s - 2):
+                store_g(s - 2)
+            if ok(s + 4) and s + 4 > 0:
+                load_x(s + 4)
+            if 4 <= s + 8 < NT:
+                load_stage((s + 8) // 4, (s + 8) % 4)
+            if ok(s + 4):
+                sort_m(s + 4, 0)
+            if ok(s + 1):
+                mean(s + 1)
+            if ok(s + 4):
+                sort_m(s + 4, 1)
+            if ok(s + 1):
+                store_x2(s + 1)
+            if s < 0:
+                for part in (2 * (s + 4), 2 * (s + 4) + 1):
+                    prep_rows(2, part, w2c, w2s)
+                    if part + 4 < 8:
+                        load_rows(fc1_w, 2, part + 4)
+            if ok(s + 3):
+                add_bias(s + 3, 0)
+                add_bias(s + 3, 1)
+            if ok(s):
+                turn_h(s, 0)
+                turn_h(s, 1)
+            if ok(s + 1):
+                squares(s + 1)
+            if ok(s):
+                turn_h(s, 2)
+                turn_h(s, 3)
+            if ok(s + 3):
+                turn_m(s + 3)
+            if ok(s):
+                weave_h(s, 0)
+            if ok(s - 1):
+                fc1(s - 1, 0)
+                fc1(s - 1, 1)
+            if ok(s + 1):
+                inv_std(s + 1)
+                normalise(s + 1, "vector")
+                normalise(s + 1, "scalar")
+            if ok(s + 3):
+                add_bias(s + 3, 2)
+                add_bias(s + 3, 3)
+            if ok(s - 1):
+                fc1(s - 1, 2)
+            if ok(s):
+                weave_h(s, 1)
+            if ok(s - 1):
+                fc1(s - 1, 3)
+            if ok(s):
+                quant_h(s)
+            if ok(s - 1):
+                for j in range(4):
+                    gelu(s - 1, j)
+            if ok(s + 2):
+                proj(s + 2, 0)
+            if ok(s + 3):
+                quant_m(s + 3)
+            if ok(s + 2):
+                proj(s + 2, 1)
+                proj(s + 2, 2)
+                proj(s + 2, 3)

@@ -18,6 +18,8 @@ P = 128
 C = 2048
 NT = 64
 EPS = 1e-5
+W2_NEXT = {1: 5, 3: 6, 4: 7}
+HEAD_TILES = 2
 
 
 def rotation_segments(shift):
@@ -74,7 +76,10 @@ def tile_swintransformerblock_pb_l_kernel(
         rows = {}
 
         def load_rows(w, key, part):
-            wr = work.tile([P, 2 * C], BF16, tag=("zs" if part % 2 == 0 else "go"))
+            if part % 2 == 0 and (key == 1 or part < 4):
+                wr = work.tile([P, 2 * C], BF16, tag="zs")
+            else:
+                wr = work.tile([P, 2 * C], BF16, tag="go", bufs=3)
             w_v = w.rearrange("(l r p) k -> l p r k", l=8, r=2, p=P)
             nc.sync.dma_start(out=wr.rearrange("p (r k) -> p r k", r=2), in_=w_v[part])
             rows[(key, part)] = wr
@@ -88,20 +93,22 @@ def tile_swintransformerblock_pb_l_kernel(
                     for u in range(2):
                         base = 1024 * r + 256 * g
                         nc.tensor.transpose(pt[:, 2 * r + u, :], ww[:, base + u : base + 256 : 2], ident[:])
-                gw = work.tile([P, C], BF16, tag="gm", align_bytes=64)
-                dst = gw[:, 0:1024].bitcast(F32).rearrange("p (r c u) -> p r c u", r=2, c=P, u=2)
-                src = pt.rearrange("p (r u) c -> p r c u", r=2, u=2)
                 if g % 2 == 0:
+                    gw = work.tile([P, C], BF16, tag="gm", align_bytes=64)
+                    rows[(key, part, g // 2)] = gw
+                half = rows[(key, part, g // 2)][:, 1024 * (g % 2) : 1024 * (g % 2 + 1)]
+                dst = half.bitcast(F32).rearrange("p (r c u) -> p r c u", r=2, c=P, u=2)
+                src = pt.rearrange("p (r u) c -> p r c u", r=2, u=2)
+                if g == 1:
                     nc.vector.tensor_copy(out=dst, in_=src)
                 else:
                     nc.scalar.copy(out=dst, in_=src)
-                rows[(key, part, g)] = gw
+                rows[(key, part, "half", g)] = half
                 if g >= 1:
                     nc.vector.quantize_mx(
-                        out=wc[:, g - 1, cols].bitcast(FP8X4), scales=ws[:, g - 1, cols],
-                        in_=rows[(key, part, g - 1)][:, 0:1024],
+                        out=wc[:, g - 1, cols].bitcast(FP8X4), scales=ws[:, g - 1, cols], in_=rows[(key, part, "half", g - 1)]
                     )
-            nc.vector.quantize_mx(out=wc[:, 3, cols].bitcast(FP8X4), scales=ws[:, 3, cols], in_=rows[(key, part, 3)][:, 0:1024])
+            nc.vector.quantize_mx(out=wc[:, 3, cols].bitcast(FP8X4), scales=ws[:, 3, cols], in_=rows[(key, part, "half", 3)])
 
         staged = {}
         x_in = {}
@@ -152,17 +159,16 @@ def tile_swintransformerblock_pb_l_kernel(
             if j == 0:
                 xb = work.tile([P, C], F32, tag="xb", bufs=3)
                 x_sum[i] = xb
-            for cols in (slice(512 * j, 512 * j + 256), slice(512 * j + 256, 512 * j + 512)):
-                nc.gpsimd.tensor_tensor(out=x_sum[i][:, cols], in0=x_in[i][:, cols], in1=ob[:, cols], op=ALU.add)
+            cols = slice(512 * j, 512 * (j + 1))
+            nc.vector.tensor_tensor(out=x_sum[i][:, cols], in0=x_in[i][:, cols], in1=ob[:, cols], op=ALU.add)
 
-        def sort_m(i, u):
-            if u == 0:
-                srt = work.tile([P, 1024], F32, tag="srt")
-                sorted_m[i] = srt
+        def sort_m(i):
+            srt = work.tile([P, 1024], F32, tag="srt")
+            sorted_m[i] = srt
             st_w = staged[i // 4].bitcast(F32).rearrange("p (a c dh u) -> p a c dh u", a=64, c=4, dh=8, u=2)
-            nc.vector.tensor_copy(
-                out=sorted_m[i].rearrange("p (u a dh) -> p u a dh", u=2, a=64, dh=8)[:, u],
-                in_=st_w[:, :, i % 4, :, u],
+            nc.scalar.copy(
+                out=srt.rearrange("p (u a dh) -> p u a dh", u=2, a=64, dh=8),
+                in_=st_w[:, :, i % 4, :, :].rearrange("p a dh u -> p u a dh"),
             )
 
         def turn_m(i):
@@ -238,27 +244,19 @@ def tile_swintransformerblock_pb_l_kernel(
             )
             rstd = work.tile([P, 1], F32, tag="rstd", bufs=3)
             nc.gpsimd.tensor_tensor(out=rstd[:], in0=ve[:], in1=mhalf[:], op=ALU.pow)
-            nmr = work.tile([P, 1], F32, tag="nmr", bufs=3)
-            nc.gpsimd.tensor_tensor(out=nmr[:], in0=rstd[:], in1=stat[(i, "negmean")][:], op=ALU.mult)
             stat[(i, "rstd")] = rstd
-            stat[(i, "nmr")] = nmr
 
-        def normalise(i, engine):
+        def normalise(i, g):
             z_v = z_srt[i].rearrange("q (g t m) -> q g t m", g=4, t=4, m=P)
             x_r = x_sum[i].rearrange("q (g m t) -> q g t m", g=4, m=P, t=4)
-            if engine == "vector":
-                nc.vector.tensor_scalar(
-                    out=z_v[:, 0:2], in0=x_r[:, 0:2], scalar1=stat[(i, "negmean")][:], scalar2=stat[(i, "rstd")][:],
-                    op0=ALU.add, op1=ALU.mult,
-                )
-            else:
-                nc.scalar.activation(
-                    out=z_v[:, 2:4], in_=x_r[:, 2:4], func=ACT.Identity, bias=stat[(i, "nmr")][:], scale=stat[(i, "rstd")][:]
-                )
+            nc.gpsimd.tensor_scalar(
+                out=z_v[:, g], in0=x_r[:, g], scalar1=stat[(i, "negmean")][:], scalar2=stat[(i, "rstd")][:],
+                op0=ALU.add, op1=ALU.mult,
+            )
 
         def turn_h(i, g):
             if g == 0:
-                ht = work.tile([P, 16, P], BF16, tag="ht")
+                ht = work.tile([P, 16, P], BF16, tag="ht", bufs=1)
                 h_t[i] = ht
             zs = z_srt[i]
             pt = psum.tile([P, 4, P], F32, tag="ps")
@@ -273,7 +271,7 @@ def tile_swintransformerblock_pb_l_kernel(
 
         def weave_h(i, half):
             if half == 0:
-                gh = work.tile([P, C], BF16, tag="gh", align_bytes=64)
+                gh = work.tile([P, C], BF16, tag="gh", bufs=1, align_bytes=64)
                 h_grp[i] = gh
             nc.vector.tensor_copy(
                 out=h_grp[i].rearrange("p (g q t) -> p g q t", g=4, q=P, t=4)[:, 2 * half : 2 * half + 2],
@@ -288,7 +286,7 @@ def tile_swintransformerblock_pb_l_kernel(
 
         def fc1(i, j):
             if j == 0:
-                go = work.tile([P, C], F32, tag="go")
+                go = work.tile([P, C], F32, tag="go", bufs=3)
                 g_out[i] = go
             hc, hs = h_q[i]
             go = g_out[i]
@@ -301,51 +299,19 @@ def tile_swintransformerblock_pb_l_kernel(
             cols = slice(512 * j, 512 * (j + 1))
             nc.scalar.activation(out=g_out[i][:, cols], in_=g_out[i][:, cols], func=ACT.Gelu)
 
-        for part in range(4):
-            load_rows(out_w, 1, part)
-        nc.sync.dma_start(out=ob[:], in_=out_b.partition_broadcast(P))
-        for part in range(8):
-            prep_rows(1, part, w1c, w1s)
-            if part + 4 < 8:
-                load_rows(out_w, 1, part + 4)
-            if part == 3:
-                for q in range(4):
-                    load_stage(0, q)
-                load_x(0)
-        nc.sync.dma_start(out=fb[:], in_=fc1_b.partition_broadcast(P))
-        nc.sync.dma_start(
-            out=wraw.rearrange("p (g t) -> p g t", g=4), in_=norm2_w.rearrange("(g p t) -> p g t", g=4, p=P, t=4)
-        )
-        nc.sync.dma_start(
-            out=braw.rearrange("p (g t) -> p g t", g=4), in_=norm2_b.rearrange("(g p t) -> p g t", g=4, p=P, t=4)
-        )
-        nc.vector.tensor_copy(out=wcol[:], in_=wraw[:])
-        nc.vector.tensor_copy(out=bcol[:], in_=braw[:])
-        for part in range(4):
-            load_rows(fc1_w, 2, part)
-
-        for s in range(-4, NT + 2):
+        def step(s, parts):
             if ok(s - 2):
                 store_g(s - 2)
-            if ok(s + 4) and s + 4 > 0:
+            if ok(s + 4) and s + 4 > HEAD_TILES:
                 load_x(s + 4)
-            if 4 <= s + 8 < NT:
+            if 8 <= s + 8 < NT:
                 load_stage((s + 8) // 4, (s + 8) % 4)
-            if ok(s + 4):
-                sort_m(s + 4, 0)
+            if ok(s + 3) and s + 3 >= HEAD_TILES:
+                add_bias(s + 3, 0)
             if ok(s + 1):
                 mean(s + 1)
-            if ok(s + 4):
-                sort_m(s + 4, 1)
-            if ok(s + 1):
                 store_x2(s + 1)
-            if s < 0:
-                for part in (2 * (s + 4), 2 * (s + 4) + 1):
-                    prep_rows(2, part, w2c, w2s)
-                    if part + 4 < 8:
-                        load_rows(fc1_w, 2, part + 4)
-            if ok(s + 3):
-                add_bias(s + 3, 0)
+            if ok(s + 3) and s + 3 >= HEAD_TILES:
                 add_bias(s + 3, 1)
             if ok(s):
                 turn_h(s, 0)
@@ -355,20 +321,24 @@ def tile_swintransformerblock_pb_l_kernel(
             if ok(s):
                 turn_h(s, 2)
                 turn_h(s, 3)
-            if ok(s + 3):
+            if ok(s + 3) and s + 3 >= HEAD_TILES:
                 turn_m(s + 3)
+            if ok(s + 4) and s + 4 > HEAD_TILES:
+                sort_m(s + 4)
             if ok(s):
                 weave_h(s, 0)
+            if ok(s + 3) and s + 3 >= HEAD_TILES:
+                add_bias(s + 3, 2)
             if ok(s - 1):
                 fc1(s - 1, 0)
+            if ok(s + 3) and s + 3 >= HEAD_TILES:
+                add_bias(s + 3, 3)
+            if ok(s - 1):
                 fc1(s - 1, 1)
             if ok(s + 1):
                 inv_std(s + 1)
-                normalise(s + 1, "vector")
-                normalise(s + 1, "scalar")
-            if ok(s + 3):
-                add_bias(s + 3, 2)
-                add_bias(s + 3, 3)
+                for g in range(4):
+                    normalise(s + 1, g)
             if ok(s - 1):
                 fc1(s - 1, 2)
             if ok(s):
@@ -380,11 +350,66 @@ def tile_swintransformerblock_pb_l_kernel(
             if ok(s - 1):
                 for j in range(4):
                     gelu(s - 1, j)
-            if ok(s + 2):
+            if ok(s + 2) and s + 2 >= HEAD_TILES:
                 proj(s + 2, 0)
-            if ok(s + 3):
+            if ok(s + 3) and s + 3 >= HEAD_TILES:
                 quant_m(s + 3)
-            if ok(s + 2):
+            if ok(s + 2) and s + 2 >= HEAD_TILES:
                 proj(s + 2, 1)
                 proj(s + 2, 2)
                 proj(s + 2, 3)
+            for part in parts:
+                prep_rows(2, part, w2c, w2s)
+                if part in W2_NEXT:
+                    load_rows(fc1_w, 2, W2_NEXT[part])
+
+        def prep_w1(part):
+            prep_rows(1, part, w1c, w1s)
+            if part < 4:
+                load_rows(out_w, 1, part + 4)
+            else:
+                load_rows(fc1_w, 2, part - 4)
+            if part == 7:
+                load_rows(fc1_w, 2, 4)
+
+        load_rows(out_w, 1, 0)
+        load_rows(out_w, 1, 1)
+        for q in range(4):
+            load_stage(0, q)
+        load_x(0)
+        nc.sync.dma_start(out=ob[:], in_=out_b.partition_broadcast(P))
+        nc.sync.dma_start(
+            out=wraw.rearrange("p (g t) -> p g t", g=4), in_=norm2_w.rearrange("(g p t) -> p g t", g=4, p=P, t=4)
+        )
+        nc.sync.dma_start(
+            out=braw.rearrange("p (g t) -> p g t", g=4), in_=norm2_b.rearrange("(g p t) -> p g t", g=4, p=P, t=4)
+        )
+        load_rows(out_w, 1, 2)
+        load_rows(out_w, 1, 3)
+        load_x(1)
+        prep_w1(0)
+        prep_w1(1)
+        load_x(2)
+        for i in range(HEAD_TILES):
+            sort_m(i)
+            for jj in range(4):
+                add_bias(i, jj)
+            turn_m(i)
+            quant_m(i)
+        sort_m(HEAD_TILES)
+        prep_w1(2)
+        for j in range(4):
+            for i in range(HEAD_TILES):
+                proj(i, j)
+            for part in (2 * j + 3, 2 * j + 4):
+                if part < 8:
+                    prep_w1(part)
+        nc.sync.dma_start(out=fb[:], in_=fc1_b.partition_broadcast(P))
+        nc.vector.tensor_copy(out=wcol[:], in_=wraw[:])
+        nc.vector.tensor_copy(out=bcol[:], in_=braw[:])
+        for q in range(4):
+            load_stage(1, q)
+        step(-1, (0, 1, 2, 3))
+        step(0, (4, 5, 6, 7))
+        for s in range(1, NT + 2):
+            step(s, ())

@@ -18,7 +18,7 @@ P = 128
 C = 2048
 NT = 64
 EPS = 1e-5
-W2_NEXT = {1: 5, 3: 6, 4: 7}
+W2_NEXT = {1: 4, 3: 5, 4: 6, 5: 7}
 HEAD_TILES = 2
 
 
@@ -76,10 +76,7 @@ def tile_swintransformerblock_pb_l_kernel(
         rows = {}
 
         def load_rows(w, key, part):
-            if part % 2 == 0 and (key == 1 or part < 4):
-                wr = work.tile([P, 2 * C], BF16, tag="zs")
-            else:
-                wr = work.tile([P, 2 * C], BF16, tag="go", bufs=3)
+            wr = work.tile([P, 2 * C], BF16, tag=("zs" if part % 2 == 0 and (key == 1 or part < 4) else "go"))
             w_v = w.rearrange("(l r p) k -> l p r k", l=8, r=2, p=P)
             nc.sync.dma_start(out=wr.rearrange("p (r k) -> p r k", r=2), in_=w_v[part])
             rows[(key, part)] = wr
@@ -159,16 +156,18 @@ def tile_swintransformerblock_pb_l_kernel(
             if j == 0:
                 xb = work.tile([P, C], F32, tag="xb", bufs=3)
                 x_sum[i] = xb
-            cols = slice(512 * j, 512 * (j + 1))
-            nc.vector.tensor_tensor(out=x_sum[i][:, cols], in0=x_in[i][:, cols], in1=ob[:, cols], op=ALU.add)
+            for cols in (slice(512 * j, 512 * j + 256), slice(512 * j + 256, 512 * j + 512)):
+                nc.gpsimd.tensor_tensor(out=x_sum[i][:, cols], in0=x_in[i][:, cols], in1=ob[:, cols], op=ALU.add)
 
-        def sort_m(i):
-            srt = work.tile([P, 1024], F32, tag="srt")
-            sorted_m[i] = srt
+        def sort_m(i, half):
+            if half == 0:
+                srt = work.tile([P, 1024], F32, tag="srt")
+                sorted_m[i] = srt
             st_w = staged[i // 4].bitcast(F32).rearrange("p (a c dh u) -> p a c dh u", a=64, c=4, dh=8, u=2)
-            nc.scalar.copy(
-                out=srt.rearrange("p (u a dh) -> p u a dh", u=2, a=64, dh=8),
-                in_=st_w[:, :, i % 4, :, :].rearrange("p a dh u -> p u a dh"),
+            heads = slice(32 * half, 32 * (half + 1))
+            nc.vector.tensor_copy(
+                out=sorted_m[i].rearrange("p (u a dh) -> p a dh u", u=2, a=64, dh=8)[:, heads],
+                in_=st_w[:, heads, i % 4, :, :],
             )
 
         def turn_m(i):
@@ -246,17 +245,18 @@ def tile_swintransformerblock_pb_l_kernel(
             nc.gpsimd.tensor_tensor(out=rstd[:], in0=ve[:], in1=mhalf[:], op=ALU.pow)
             stat[(i, "rstd")] = rstd
 
-        def normalise(i, g):
-            z_v = z_srt[i].rearrange("q (g t m) -> q g t m", g=4, t=4, m=P)
-            x_r = x_sum[i].rearrange("q (g m t) -> q g t m", g=4, m=P, t=4)
-            nc.gpsimd.tensor_scalar(
-                out=z_v[:, g], in0=x_r[:, g], scalar1=stat[(i, "negmean")][:], scalar2=stat[(i, "rstd")][:],
+        def normalise(i, half):
+            z_v = z_srt[i].rearrange("q (g t m) -> q g m t", g=4, t=4, m=P)
+            x_r = x_sum[i].rearrange("q (g m t) -> q g m t", g=4, m=P, t=4)
+            gs = slice(2 * half, 2 * half + 2)
+            nc.vector.tensor_scalar(
+                out=z_v[:, gs], in0=x_r[:, gs], scalar1=stat[(i, "negmean")][:], scalar2=stat[(i, "rstd")][:],
                 op0=ALU.add, op1=ALU.mult,
             )
 
         def turn_h(i, g):
             if g == 0:
-                ht = work.tile([P, 16, P], BF16, tag="ht", bufs=1)
+                ht = work.tile([P, 16, P], BF16, tag="ht")
                 h_t[i] = ht
             zs = z_srt[i]
             pt = psum.tile([P, 4, P], F32, tag="ps")
@@ -271,7 +271,7 @@ def tile_swintransformerblock_pb_l_kernel(
 
         def weave_h(i, half):
             if half == 0:
-                gh = work.tile([P, C], BF16, tag="gh", bufs=1, align_bytes=64)
+                gh = work.tile([P, C], BF16, tag="gh", align_bytes=64)
                 h_grp[i] = gh
             nc.vector.tensor_copy(
                 out=h_grp[i].rearrange("p (g q t) -> p g q t", g=4, q=P, t=4)[:, 2 * half : 2 * half + 2],
@@ -286,7 +286,7 @@ def tile_swintransformerblock_pb_l_kernel(
 
         def fc1(i, j):
             if j == 0:
-                go = work.tile([P, C], F32, tag="go", bufs=3)
+                go = work.tile([P, C], F32, tag="go")
                 g_out[i] = go
             hc, hs = h_q[i]
             go = g_out[i]
@@ -306,13 +306,13 @@ def tile_swintransformerblock_pb_l_kernel(
                 load_x(s + 4)
             if 8 <= s + 8 < NT:
                 load_stage((s + 8) // 4, (s + 8) % 4)
-            if ok(s + 3) and s + 3 >= HEAD_TILES:
-                add_bias(s + 3, 0)
+            if ok(s + 4) and s + 4 > HEAD_TILES:
+                sort_m(s + 4, 0)
             if ok(s + 1):
                 mean(s + 1)
                 store_x2(s + 1)
-            if ok(s + 3) and s + 3 >= HEAD_TILES:
-                add_bias(s + 3, 1)
+            if ok(s + 4) and s + 4 > HEAD_TILES:
+                sort_m(s + 4, 1)
             if ok(s):
                 turn_h(s, 0)
                 turn_h(s, 1)
@@ -323,24 +323,21 @@ def tile_swintransformerblock_pb_l_kernel(
                 turn_h(s, 3)
             if ok(s + 3) and s + 3 >= HEAD_TILES:
                 turn_m(s + 3)
-            if ok(s + 4) and s + 4 > HEAD_TILES:
-                sort_m(s + 4)
             if ok(s):
                 weave_h(s, 0)
-            if ok(s + 3) and s + 3 >= HEAD_TILES:
-                add_bias(s + 3, 2)
             if ok(s - 1):
                 fc1(s - 1, 0)
-            if ok(s + 3) and s + 3 >= HEAD_TILES:
-                add_bias(s + 3, 3)
-            if ok(s - 1):
                 fc1(s - 1, 1)
             if ok(s + 1):
                 inv_std(s + 1)
-                for g in range(4):
-                    normalise(s + 1, g)
+                normalise(s + 1, 0)
+            if ok(s + 3) and s + 3 >= HEAD_TILES:
+                for j in range(4):
+                    add_bias(s + 3, j)
             if ok(s - 1):
                 fc1(s - 1, 2)
+            if ok(s + 1):
+                normalise(s + 1, 1)
             if ok(s):
                 weave_h(s, 1)
             if ok(s - 1):
@@ -369,8 +366,6 @@ def tile_swintransformerblock_pb_l_kernel(
                 load_rows(out_w, 1, part + 4)
             else:
                 load_rows(fc1_w, 2, part - 4)
-            if part == 7:
-                load_rows(fc1_w, 2, 4)
 
         load_rows(out_w, 1, 0)
         load_rows(out_w, 1, 1)
@@ -391,12 +386,14 @@ def tile_swintransformerblock_pb_l_kernel(
         prep_w1(1)
         load_x(2)
         for i in range(HEAD_TILES):
-            sort_m(i)
+            sort_m(i, 0)
+            sort_m(i, 1)
             for jj in range(4):
                 add_bias(i, jj)
             turn_m(i)
             quant_m(i)
-        sort_m(HEAD_TILES)
+        sort_m(HEAD_TILES, 0)
+        sort_m(HEAD_TILES, 1)
         prep_w1(2)
         for j in range(4):
             for i in range(HEAD_TILES):

@@ -20,6 +20,8 @@ NT = 64
 EPS = 1e-5
 W2_NEXT = {1: 4, 3: 5, 4: 6, 5: 7}
 HEAD_TILES = 2
+XB_PIECE = 256
+NZ_VECTOR = 1
 
 
 def rotation_segments(shift):
@@ -156,7 +158,8 @@ def tile_swintransformerblock_pb_l_kernel(
             if j == 0:
                 xb = work.tile([P, C], F32, tag="xb", bufs=3)
                 x_sum[i] = xb
-            for cols in (slice(512 * j, 512 * j + 256), slice(512 * j + 256, 512 * j + 512)):
+            for c0 in range(512 * j, 512 * (j + 1), XB_PIECE):
+                cols = slice(c0, c0 + XB_PIECE)
                 nc.gpsimd.tensor_tensor(out=x_sum[i][:, cols], in0=x_in[i][:, cols], in1=ob[:, cols], op=ALU.add)
 
         def sort_m(i, half):
@@ -243,16 +246,25 @@ def tile_swintransformerblock_pb_l_kernel(
             )
             rstd = work.tile([P, 1], F32, tag="rstd", bufs=3)
             nc.gpsimd.tensor_tensor(out=rstd[:], in0=ve[:], in1=mhalf[:], op=ALU.pow)
+            nmr = work.tile([P, 1], F32, tag="nmr", bufs=3)
+            nc.gpsimd.tensor_tensor(out=nmr[:], in0=rstd[:], in1=stat[(i, "negmean")][:], op=ALU.mult)
             stat[(i, "rstd")] = rstd
+            stat[(i, "nmr")] = nmr
 
         def normalise(i, half):
             z_v = z_srt[i].rearrange("q (g t m) -> q g m t", g=4, t=4, m=P)
             x_r = x_sum[i].rearrange("q (g m t) -> q g m t", g=4, m=P, t=4)
-            gs = slice(2 * half, 2 * half + 2)
-            nc.vector.tensor_scalar(
-                out=z_v[:, gs], in0=x_r[:, gs], scalar1=stat[(i, "negmean")][:], scalar2=stat[(i, "rstd")][:],
-                op0=ALU.add, op1=ALU.mult,
-            )
+            if half == 0:
+                gs = slice(0, NZ_VECTOR)
+                nc.vector.tensor_scalar(
+                    out=z_v[:, gs], in0=x_r[:, gs], scalar1=stat[(i, "negmean")][:], scalar2=stat[(i, "rstd")][:],
+                    op0=ALU.add, op1=ALU.mult,
+                )
+            else:
+                gs = slice(NZ_VECTOR, 4)
+                nc.scalar.activation(
+                    out=z_v[:, gs], in_=x_r[:, gs], func=ACT.Identity, bias=stat[(i, "nmr")][:], scale=stat[(i, "rstd")][:]
+                )
 
         def turn_h(i, g):
             if g == 0:

@@ -20,8 +20,10 @@ NT = 64
 EPS = 1e-5
 W2_NEXT = {1: 4, 3: 5, 4: 6, 5: 7}
 HEAD_TILES = 2
+LAG = 1
+XB_VECTOR = 2
 XB_PIECE = 256
-NZ_VECTOR = 1
+C2_VECTOR = 1
 
 
 def rotation_segments(shift):
@@ -74,6 +76,22 @@ def tile_swintransformerblock_pb_l_kernel(
         braw = keep.tile([P, 16], BF16, name="braw")
         wcol = keep.tile([P, 16], F32, name="wcol")
         bcol = keep.tile([P, 16], F32, name="bcol")
+
+        ones = keep.tile([P, P], BF16, name="ones")
+        nc.vector.memset(ones[:], 1.0)
+
+        def load_bias_row(vec):
+            brow = work.tile([P, C], BF16, tag="gh", align_bytes=64)
+            nc.vector.memset(brow[:], 0.0)
+            nc.sync.dma_start(out=brow[0:1, :], in_=vec.rearrange("(o c) -> o c", o=1))
+            return brow
+
+        def spread_bias(brow, dst):
+            for j in range(4):
+                cols = slice(512 * j, 512 * (j + 1))
+                ps = psum.tile([P, 512], F32, tag="ps")
+                nc.tensor.matmul(out=ps[:], lhsT=ones[:], rhs=brow[:, cols], start=True, stop=True)
+                nc.scalar.copy(out=dst[:, cols], in_=ps[:])
 
         rows = {}
 
@@ -158,9 +176,13 @@ def tile_swintransformerblock_pb_l_kernel(
             if j == 0:
                 xb = work.tile([P, C], F32, tag="xb", bufs=3)
                 x_sum[i] = xb
-            for c0 in range(512 * j, 512 * (j + 1), XB_PIECE):
-                cols = slice(c0, c0 + XB_PIECE)
-                nc.gpsimd.tensor_tensor(out=x_sum[i][:, cols], in0=x_in[i][:, cols], in1=ob[:, cols], op=ALU.add)
+            piece = XB_PIECE if j >= XB_VECTOR else 512
+            for c0 in range(512 * j, 512 * (j + 1), piece):
+                cols = slice(c0, c0 + piece)
+                if j >= XB_VECTOR:
+                    nc.gpsimd.tensor_tensor(out=x_sum[i][:, cols], in0=x_in[i][:, cols], in1=ob[:, cols], op=ALU.add)
+                else:
+                    nc.vector.tensor_tensor(out=x_sum[i][:, cols], in0=x_in[i][:, cols], in1=ob[:, cols], op=ALU.add)
 
         def sort_m(i, half):
             if half == 0:
@@ -251,20 +273,12 @@ def tile_swintransformerblock_pb_l_kernel(
             stat[(i, "rstd")] = rstd
             stat[(i, "nmr")] = nmr
 
-        def normalise(i, half):
+        def normalise(i):
             z_v = z_srt[i].rearrange("q (g t m) -> q g m t", g=4, t=4, m=P)
             x_r = x_sum[i].rearrange("q (g m t) -> q g m t", g=4, m=P, t=4)
-            if half == 0:
-                gs = slice(0, NZ_VECTOR)
-                nc.vector.tensor_scalar(
-                    out=z_v[:, gs], in0=x_r[:, gs], scalar1=stat[(i, "negmean")][:], scalar2=stat[(i, "rstd")][:],
-                    op0=ALU.add, op1=ALU.mult,
-                )
-            else:
-                gs = slice(NZ_VECTOR, 4)
-                nc.scalar.activation(
-                    out=z_v[:, gs], in_=x_r[:, gs], func=ACT.Identity, bias=stat[(i, "nmr")][:], scale=stat[(i, "rstd")][:]
-                )
+            nc.scalar.activation(
+                out=z_v, in_=x_r, func=ACT.Identity, bias=stat[(i, "nmr")][:], scale=stat[(i, "rstd")][:]
+            )
 
         def turn_h(i, g):
             if g == 0:
@@ -277,9 +291,15 @@ def tile_swintransformerblock_pb_l_kernel(
                 nc.tensor.transpose(pt[:, t, :], zs[:, P * k : P * (k + 1)], ident[:])
             for t in range(4):
                 k = 4 * g + t
-                nc.scalar.activation(
-                    out=h_t[i][:, k, :], in_=pt[:, t, :], func=ACT.Identity, bias=bcol[:, k : k + 1], scale=wcol[:, k : k + 1]
-                )
+                if g >= 4 - C2_VECTOR:
+                    nc.vector.tensor_scalar(
+                        out=h_t[i][:, k, :], in0=pt[:, t, :], scalar1=wcol[:, k : k + 1], scalar2=bcol[:, k : k + 1],
+                        op0=ALU.mult, op1=ALU.add,
+                    )
+                else:
+                    nc.scalar.activation(
+                        out=h_t[i][:, k, :], in_=pt[:, t, :], func=ACT.Identity, bias=bcol[:, k : k + 1], scale=wcol[:, k : k + 1]
+                    )
 
         def weave_h(i, half):
             if half == 0:
@@ -291,8 +311,8 @@ def tile_swintransformerblock_pb_l_kernel(
             )
 
         def quant_h(i):
-            hc = work.tile([P, 512], U32, tag="hc", align_bytes=64)
-            hs = work.tile([P, 512], U8, tag="hs", align_bytes=64)
+            hc = work.tile([P, 512], U32, tag="hc", bufs=2 + LAG, align_bytes=64)
+            hs = work.tile([P, 512], U8, tag="hs", bufs=2 + LAG, align_bytes=64)
             nc.vector.quantize_mx(out=hc.bitcast(FP8X4), scales=hs[:], in_=h_grp[i][:])
             h_q[i] = (hc, hs)
 
@@ -312,8 +332,8 @@ def tile_swintransformerblock_pb_l_kernel(
             nc.scalar.activation(out=g_out[i][:, cols], in_=g_out[i][:, cols], func=ACT.Gelu)
 
         def step(s, parts):
-            if ok(s - 2):
-                store_g(s - 2)
+            if ok(s - 2 - LAG):
+                store_g(s - 2 - LAG)
             if ok(s + 4) and s + 4 > HEAD_TILES:
                 load_x(s + 4)
             if 8 <= s + 8 < NT:
@@ -337,28 +357,27 @@ def tile_swintransformerblock_pb_l_kernel(
                 turn_m(s + 3)
             if ok(s):
                 weave_h(s, 0)
-            if ok(s - 1):
-                fc1(s - 1, 0)
-                fc1(s - 1, 1)
+            if ok(s - 1 - LAG):
+                fc1(s - 1 - LAG, 0)
+                fc1(s - 1 - LAG, 1)
             if ok(s + 1):
                 inv_std(s + 1)
-                normalise(s + 1, 0)
             if ok(s + 3) and s + 3 >= HEAD_TILES:
                 for j in range(4):
                     add_bias(s + 3, j)
-            if ok(s - 1):
-                fc1(s - 1, 2)
+            if ok(s - 1 - LAG):
+                fc1(s - 1 - LAG, 2)
             if ok(s + 1):
-                normalise(s + 1, 1)
+                normalise(s + 1)
             if ok(s):
                 weave_h(s, 1)
-            if ok(s - 1):
-                fc1(s - 1, 3)
+            if ok(s - 1 - LAG):
+                fc1(s - 1 - LAG, 3)
             if ok(s):
                 quant_h(s)
-            if ok(s - 1):
+            if ok(s - 1 - LAG):
                 for j in range(4):
-                    gelu(s - 1, j)
+                    gelu(s - 1 - LAG, j)
             if ok(s + 2) and s + 2 >= HEAD_TILES:
                 proj(s + 2, 0)
             if ok(s + 3) and s + 3 >= HEAD_TILES:
@@ -381,21 +400,18 @@ def tile_swintransformerblock_pb_l_kernel(
 
         load_rows(out_w, 1, 0)
         load_rows(out_w, 1, 1)
+        ob_row = load_bias_row(out_b)
+        fb_row = load_bias_row(fc1_b)
         for q in range(4):
             load_stage(0, q)
         load_x(0)
-        nc.sync.dma_start(out=ob[:], in_=out_b.partition_broadcast(P))
-        nc.sync.dma_start(
-            out=wraw.rearrange("p (g t) -> p g t", g=4), in_=norm2_w.rearrange("(g p t) -> p g t", g=4, p=P, t=4)
-        )
-        nc.sync.dma_start(
-            out=braw.rearrange("p (g t) -> p g t", g=4), in_=norm2_b.rearrange("(g p t) -> p g t", g=4, p=P, t=4)
-        )
         load_rows(out_w, 1, 2)
         load_rows(out_w, 1, 3)
         load_x(1)
         prep_w1(0)
         prep_w1(1)
+        spread_bias(ob_row, ob)
+        spread_bias(fb_row, fb)
         load_x(2)
         for i in range(HEAD_TILES):
             sort_m(i, 0)
@@ -413,12 +429,18 @@ def tile_swintransformerblock_pb_l_kernel(
             for part in (2 * j + 3, 2 * j + 4):
                 if part < 8:
                     prep_w1(part)
-        nc.sync.dma_start(out=fb[:], in_=fc1_b.partition_broadcast(P))
+        nc.sync.dma_start(
+            out=wraw.rearrange("p (g t) -> p g t", g=4), in_=norm2_w.rearrange("(g p t) -> p g t", g=4, p=P, t=4)
+        )
+        nc.sync.dma_start(
+            out=braw.rearrange("p (g t) -> p g t", g=4), in_=norm2_b.rearrange("(g p t) -> p g t", g=4, p=P, t=4)
+        )
         nc.vector.tensor_copy(out=wcol[:], in_=wraw[:])
         nc.vector.tensor_copy(out=bcol[:], in_=braw[:])
         for q in range(4):
             load_stage(1, q)
-        step(-1, (0, 1, 2, 3))
-        step(0, (4, 5, 6, 7))
-        for s in range(1, NT + 2):
+        step(-1, (0, 1, 2))
+        step(0, (3, 4, 5))
+        step(1, (6, 7))
+        for s in range(2, NT + 2 + LAG):
             step(s, ())

from contextlib import ExitStack

import concourse.mybir as mybir
from concourse.masks import make_identity

FLOPS = 2 * 2 * 8192 * 2048 * 2048

F32 = mybir.dt.float32
BF16 = mybir.dt.bfloat16
U32 = mybir.dt.uint32
U8 = mybir.dt.uint8
FP8X4 = mybir.dt.float8_e4m3fn_x4
ALU = mybir.AluOpType
ACT = mybir.ActivationFunctionType
AX = mybir.AxisListType

P = 128
C = 2048
NT = 64
EPS = 1e-5
W2_NEXT = {1: 4, 3: 5, 4: 6, 5: 7}
HEAD_TILES = 2
LAG = 1
XB_VECTOR = 2
XB_PIECE = 256
C2_VECTOR = 1


def rotation_segments(shift):
    if shift == 0:
        return [(0, 4, 0, 4)]
    return [(1, 4, 0, 3), (0, 1, 3, 4)]


def tile_swintransformerblock_pb_l_kernel(
    tc, o_heads, x, out_w, out_b, norm2_w, norm2_b, fc1_w, fc1_b, out_0, out_1
):
    nc = tc.nc
    with ExitStack() as ctx:
        keep = ctx.enter_context(tc.tile_pool(name="keep", bufs=1))
        work = ctx.enter_context(tc.tile_pool(name="work", bufs=2))
        psum = ctx.enter_context(tc.psum_pool(name="psum", bufs=8))
        ctx.enter_context(tc.manual_schedule())

        grid = "b (iw ri jw cj) ch -> (b iw) ri jw cj ch"
        x_v = x.rearrange(grid, iw=4, ri=8, jw=4, cj=8)
        x2_v = out_0.rearrange(grid, iw=4, ri=8, jw=4, cj=8)
        g_v = out_1.rearrange(grid, iw=4, ri=8, jw=4, cj=8)
        oh_v = o_heads.rearrange("n a s d -> n a (s d)")

        warm = keep.tile([P, 1], F32, name="warm")
        nc.vector.memset(warm[:], 0.0)
        nc.scalar.activation(out=warm[:], in_=warm[:], func=ACT.Gelu)
        mhalf = keep.tile([P, 1], F32, name="mhalf")
        nc.vector.memset(mhalf[:], -0.5)

        ident = keep.tile([P, P], F32, name="ident")
        make_identity(nc, ident[:])
        ident_v = ident.rearrange("n (b i j) -> n b i j", b=8, i=4, j=4)
        perm = {(0, 0): ident}
        for dr, dc in ((0, 1), (1, 0), (1, 1)):
            pm = keep.tile([P, P], F32, name="perm%d%d" % (dr, dc))
            pm_v = pm.rearrange("n (b i j) -> n b i j", b=8, i=4, j=4)
            for i0, i1, s0, s1 in rotation_segments(dr):
                for j0, j1, t0, t1 in rotation_segments(dc):
                    nc.vector.tensor_copy(out=pm_v[:, :, i0:i1, j0:j1], in_=ident_v[:, :, s0:s1, t0:t1])
            perm[(dr, dc)] = pm

        w1c = keep.tile([P, 4, C], U32, name="w1c", align_bytes=64)
        w1s = keep.tile([P, 4, C], U8, name="w1s", align_bytes=64)
        w2c = keep.tile([P, 4, C], U32, name="w2c", align_bytes=64)
        w2s = keep.tile([P, 4, C], U8, name="w2s", align_bytes=64)
        ob = keep.tile([P, C], BF16, name="ob")
        fb = keep.tile([P, C], BF16, name="fb")
        wraw = keep.tile([P, 16], BF16, name="wraw")
        braw = keep.tile([P, 16], BF16, name="braw")
        wcol = keep.tile([P, 16], F32, name="wcol")
        bcol = keep.tile([P, 16], F32, name="bcol")

        ones = keep.tile([P, P], BF16, name="ones")
        nc.vector.memset(ones[:], 1.0)

        def load_bias_row(vec):
            brow = work.tile([P, C], BF16, tag="gh", align_bytes=64)
            nc.vector.memset(brow[:], 0.0)
            nc.sync.dma_start(out=brow[0:1, :], in_=vec.rearrange("(o c) -> o c", o=1))
            return brow

        def spread_bias(brow, dst):
            for j in range(4):
                cols = slice(512 * j, 512 * (j + 1))
                ps = psum.tile([P, 512], F32, tag="ps")
                nc.tensor.matmul(out=ps[:], lhsT=ones[:], rhs=brow[:, cols], start=True, stop=True)
                nc.scalar.copy(out=dst[:, cols], in_=ps[:])

        rows = {}

        def load_rows(w, key, part):
            wr = work.tile([P, 2 * C], BF16, tag=("zs" if part % 2 == 0 and (key == 1 or part < 4) else "go"))
            w_v = w.rearrange("(l r p) k -> l p r k", l=8, r=2, p=P)
            nc.sync.dma_start(out=wr.rearrange("p (r k) -> p r k", r=2), in_=w_v[part])
            rows[(key, part)] = wr

        def prep_rows(key, part, wc, ws):
            ww = rows[(key, part)].bitcast(F32)
            cols = slice(256 * part, 256 * (part + 1))
            for g in range(4):
                pt = psum.tile([P, 4, P], F32, tag="ps")
                for r in range(2):
                    for u in range(2):
                        base = 1024 * r + 256 * g
                        nc.tensor.transpose(pt[:, 2 * r + u, :], ww[:, base + u : base + 256 : 2], ident[:])
                if g % 2 == 0:
                    gw = work.tile([P, C], BF16, tag="gm", align_bytes=64)
                    rows[(key, part, g // 2)] = gw
                half = rows[(key, part, g // 2)][:, 1024 * (g % 2) : 1024 * (g % 2 + 1)]
                dst = half.bitcast(F32).rearrange("p (r c u) -> p r c u", r=2, c=P, u=2)
                src = pt.rearrange("p (r u) c -> p r c u", r=2, u=2)
                if g == 1:
                    nc.vector.tensor_copy(out=dst, in_=src)
                else:
                    nc.scalar.copy(out=dst, in_=src)
                rows[(key, part, "half", g)] = half
                if g >= 1:
                    nc.vector.quantize_mx(
                        out=wc[:, g - 1, cols].bitcast(FP8X4), scales=ws[:, g - 1, cols], in_=rows[(key, part, "half", g - 1)]
                    )
            nc.vector.quantize_mx(out=wc[:, 3, cols].bitcast(FP8X4), scales=ws[:, 3, cols], in_=rows[(key, part, "half", 3)])

        staged = {}
        x_in = {}
        x_sum = {}
        sorted_m = {}
        m_grp = {}
        m_q = {}
        stat = {}
        z_srt = {}
        h_t = {}
        h_grp = {}
        h_q = {}
        g_out = {}

        def ok(i):
            return 0 <= i < NT

        def place(i):
            return (i // 8 + 3) % 8, (i % 8 + 3) % 8

        def load_stage(grp, q):
            if q == 0:
                st = work.tile([P, 4 * C], BF16, tag="st")
                staged[grp] = st
            st_v = staged[grp].rearrange("p (a e) -> p a e", a=64)
            off = 128 * grp
            heads = slice(16 * q, 16 * (q + 1))
            nc.sync.dma_start(out=st_v[:, heads, :], in_=oh_v[:, heads, off : off + 128])

        def load_x(i):
            ri, cj = place(i)
            xt = work.tile([P, C], BF16, tag="xt", bufs=3)
            for jw in range(4):
                nc.sync.dma_start(out=xt[jw:P:4, :], in_=x_v[:, ri, jw, cj, :])
            x_in[i] = xt

        def store_x2(i):
            ri, cj = place(i)
            for jw in range(4):
                nc.sync.dma_start(out=x2_v[:, ri, jw, cj, :], in_=x_sum[i][jw:P:4, :])

        def store_g(i):
            ri, cj = place(i)
            for jw in range(4):
                nc.sync.dma_start(out=g_v[:, ri, jw, cj, :], in_=g_out[i][jw:P:4, :])

        def add_bias(i, j):
            if j == 0:
                xb = work.tile([P, C], F32, tag="xb", bufs=3)
                x_sum[i] = xb
            piece = XB_PIECE if j >= XB_VECTOR else 512
            for c0 in range(512 * j, 512 * (j + 1), piece):
                cols = slice(c0, c0 + piece)
                if j >= XB_VECTOR:
                    nc.gpsimd.tensor_tensor(out=x_sum[i][:, cols], in0=x_in[i][:, cols], in1=ob[:, cols], op=ALU.add)
                else:
                    nc.vector.tensor_tensor(out=x_sum[i][:, cols], in0=x_in[i][:, cols], in1=ob[:, cols], op=ALU.add)

        def sort_m(i, half):
            if half == 0:
                srt = work.tile([P, 1024], F32, tag="srt")
                sorted_m[i] = srt
            st_w = staged[i // 4].bitcast(F32).rearrange("p (a c dh u) -> p a c dh u", a=64, c=4, dh=8, u=2)
            heads = slice(32 * half, 32 * (half + 1))
            nc.vector.tensor_copy(
                out=sorted_m[i].rearrange("p (u a dh) -> p a dh u", u=2, a=64, dh=8)[:, heads],
                in_=st_w[:, heads, i % 4, :, :],
            )

        def turn_m(i):
            srt = sorted_m[i]
            pm = perm[((i // 8 + 3) // 8, (i % 8 + 3) // 8)]
            gm = work.tile([P, C], BF16, tag="gm", align_bytes=64)
            gm_v = gm.bitcast(F32).rearrange("p (j gg q u) -> p j gg q u", j=2, gg=2, q=P, u=2)
            for j in range(2):
                pt = psum.tile([P, 4, P], F32, tag="ps")
                for gg in range(2):
                    for u in range(2):
                        col = 512 * u + 128 * (2 * j + gg)
                        nc.tensor.transpose(pt[:, 2 * gg + u, :], srt[:, col : col + 128], pm[:])
                nc.scalar.copy(out=gm_v[:, j], in_=pt.rearrange("p (gg u) q -> p gg q u", gg=2, u=2))
            m_grp[i] = gm

        def quant_m(i):
            mc = work.tile([P, 512], U32, tag="mc", align_bytes=64)
            ms = work.tile([P, 512], U8, tag="ms", align_bytes=64)
            nc.vector.quantize_mx(out=mc.bitcast(FP8X4), scales=ms[:], in_=m_grp[i][:])
            m_q[i] = (mc, ms)

        def mx_chunk(ps, ac, asc, wc, ws, j):
            cols = slice(512 * j, 512 * (j + 1))
            for g in range(4):
                tok = slice(P * g, P * (g + 1))
                nc.tensor.matmul_mx(
                    out=ps[:],
                    lhsT=ac[:, tok].bitcast(FP8X4),
                    lhsT_scale=asc[:, tok],
                    rhs=wc[:, g, cols].bitcast(FP8X4),
                    rhs_scale=ws[:, g, cols],
                    start=(g == 0),
                    stop=(g == 3),
                )

        def proj(i, j):
            if j == 0:
                sums = work.tile([P, 4], F32, tag="sums", bufs=3)
                stat[(i, "sums")] = sums
            mc, ms = m_q[i]
            xb = x_sum[i]
            cols = slice(512 * j, 512 * (j + 1))
            ps = psum.tile([P, 512], F32, tag="ps")
            mx_chunk(ps, mc, ms, w1c, w1s, j)
            nc.vector.scalar_tensor_tensor(
                out=xb[:, cols], in0=ps[:], scalar=1.0, in1=xb[:, cols], op0=ALU.mult, op1=ALU.add,
                accum_out=stat[(i, "sums")][:, j : j + 1],
            )

        def mean(i):
            part = work.tile([P, 4], F32, tag="part", bufs=3)
            negmean = work.tile([P, 1], F32, tag="negmean", bufs=3)
            nc.vector.tensor_scalar(
                out=part[:], in0=stat[(i, "sums")][:], scalar1=-1.0 / C, scalar2=None, op0=ALU.mult, op1=ALU.add,
                accum_out=negmean[:],
            )
            stat[(i, "negmean")] = negmean

        def squares(i):
            zs = work.tile([P, C], F32, tag="zs")
            ssq = work.tile([P, 1], F32, tag="ssq", bufs=3)
            nc.scalar.activation(
                out=zs[:], in_=x_sum[i][:], func=ACT.Square, bias=stat[(i, "negmean")][:], scale=1.0, accum_out=ssq[:]
            )
            z_srt[i] = zs
            stat[(i, "ssq")] = ssq

        def inv_std(i):
            ve = work.tile([P, 1], F32, tag="ve", bufs=3)
            nc.gpsimd.tensor_scalar(
                out=ve[:], in0=stat[(i, "ssq")][:], scalar1=1.0 / C, scalar2=EPS, op0=ALU.mult, op1=ALU.add
            )
            rstd = work.tile([P, 1], F32, tag="rstd", bufs=3)
            nc.gpsimd.tensor_tensor(out=rstd[:], in0=ve[:], in1=mhalf[:], op=ALU.pow)
            nmr = work.tile([P, 1], F32, tag="nmr", bufs=3)
            nc.gpsimd.tensor_tensor(out=nmr[:], in0=rstd[:], in1=stat[(i, "negmean")][:], op=ALU.mult)
            stat[(i, "rstd")] = rstd
            stat[(i, "nmr")] = nmr

        def normalise(i):
            z_v = z_srt[i].rearrange("q (g t m) -> q g m t", g=4, t=4, m=P)
            x_r = x_sum[i].rearrange("q (g m t) -> q g m t", g=4, m=P, t=4)
            nc.scalar.activation(
                out=z_v, in_=x_r, func=ACT.Identity, bias=stat[(i, "nmr")][:], scale=stat[(i, "rstd")][:]
            )

        def turn_h(i, g):
            if g == 0:
                ht = work.tile([P, 16, P], BF16, tag="ht")
                h_t[i] = ht
            zs = z_srt[i]
            pt = psum.tile([P, 4, P], F32, tag="ps")
            for t in range(4):
                k = 4 * g + t
                nc.tensor.transpose(pt[:, t, :], zs[:, P * k : P * (k + 1)], ident[:])
            for t in range(4):
                k = 4 * g + t
                if g >= 4 - C2_VECTOR:
                    nc.vector.tensor_scalar(
                        out=h_t[i][:, k, :], in0=pt[:, t, :], scalar1=wcol[:, k : k + 1], scalar2=bcol[:, k : k + 1],
                        op0=ALU.mult, op1=ALU.add,
                    )
                else:
                    nc.scalar.activation(
                        out=h_t[i][:, k, :], in_=pt[:, t, :], func=ACT.Identity, bias=bcol[:, k : k + 1], scale=wcol[:, k : k + 1]
                    )

        def weave_h(i, half):
            if half == 0:
                gh = work.tile([P, C], BF16, tag="gh", align_bytes=64)
                h_grp[i] = gh
            nc.vector.tensor_copy(
                out=h_grp[i].rearrange("p (g q t) -> p g q t", g=4, q=P, t=4)[:, 2 * half : 2 * half + 2],
                in_=h_t[i].rearrange("p (g t) q -> p g q t", g=4, t=4)[:, 2 * half : 2 * half + 2],
            )

        def quant_h(i):
            hc = work.tile([P, 512], U32, tag="hc", bufs=2 + LAG, align_bytes=64)
            hs = work.tile([P, 512], U8, tag="hs", bufs=2 + LAG, align_bytes=64)
            nc.vector.quantize_mx(out=hc.bitcast(FP8X4), scales=hs[:], in_=h_grp[i][:])
            h_q[i] = (hc, hs)

        def fc1(i, j):
            if j == 0:
                go = work.tile([P, C], F32, tag="go")
                g_out[i] = go
            hc, hs = h_q[i]
            go = g_out[i]
            cols = slice(512 * j, 512 * (j + 1))
            ps = psum.tile([P, 512], F32, tag="ps")
            mx_chunk(ps, hc, hs, w2c, w2s, j)
            nc.vector.tensor_tensor(out=go[:, cols], in0=ps[:], in1=fb[:, cols], op=ALU.add)

        def gelu(i, j):
            cols = slice(512 * j, 512 * (j + 1))
            nc.scalar.activation(out=g_out[i][:, cols], in_=g_out[i][:, cols], func=ACT.Gelu)

        def step(s, parts):
            if ok(s - 2 - LAG):
                store_g(s - 2 - LAG)
            if ok(s + 4) and s + 4 > HEAD_TILES:
                load_x(s + 4)
            if 8 <= s + 8 < NT:
                load_stage((s + 8) // 4, (s + 8) % 4)
            if ok(s + 4) and s + 4 > HEAD_TILES:
                sort_m(s + 4, 0)
            if ok(s + 1):
                mean(s + 1)
                store_x2(s + 1)
            if ok(s + 4) and s + 4 > HEAD_TILES:
                sort_m(s + 4, 1)
            if ok(s):
                turn_h(s, 0)
                turn_h(s, 1)
            if ok(s + 1):
                squares(s + 1)
            if ok(s):
                turn_h(s, 2)
                turn_h(s, 3)
            if ok(s + 3) and s + 3 >= HEAD_TILES:
                turn_m(s + 3)
            if ok(s):
                weave_h(s, 0)
            if ok(s - 1 - LAG):
                fc1(s - 1 - LAG, 0)
                fc1(s - 1 - LAG, 1)
            if ok(s + 1):
                inv_std(s + 1)
            if ok(s + 3) and s + 3 >= HEAD_TILES:
                for j in range(4):
                    add_bias(s + 3, j)
            if ok(s - 1 - LAG):
                fc1(s - 1 - LAG, 2)
            if ok(s + 1):
                normalise(s + 1)
            if ok(s):
                weave_h(s, 1)
            if ok(s - 1 - LAG):
                fc1(s - 1 - LAG, 3)
            if ok(s):
                quant_h(s)
            if ok(s - 1 - LAG):
                for j in range(4):
                    gelu(s - 1 - LAG, j)
            if ok(s + 2) and s + 2 >= HEAD_TILES:
                proj(s + 2, 0)
            if ok(s + 3) and s + 3 >= HEAD_TILES:
                quant_m(s + 3)
            if ok(s + 2) and s + 2 >= HEAD_TILES:
                proj(s + 2, 1)
                proj(s + 2, 2)
                proj(s + 2, 3)
            for part in parts:
                prep_rows(2, part, w2c, w2s)
                if part in W2_NEXT:
                    load_rows(fc1_w, 2, W2_NEXT[part])

        def prep_w1(part):
            prep_rows(1, part, w1c, w1s)
            if part < 4:
                load_rows(out_w, 1, part + 4)
            else:
                load_rows(fc1_w, 2, part - 4)

        load_rows(out_w, 1, 0)
        load_rows(out_w, 1, 1)
        ob_row = load_bias_row(out_b)
        fb_row = load_bias_row(fc1_b)
        for q in range(4):
            load_stage(0, q)
        load_x(0)
        load_rows(out_w, 1, 2)
        load_rows(out_w, 1, 3)
        load_x(1)
        prep_w1(0)
        prep_w1(1)
        spread_bias(ob_row, ob)
        spread_bias(fb_row, fb)
        load_x(2)
        for i in range(HEAD_TILES):
            sort_m(i, 0)
            sort_m(i, 1)
            for jj in range(4):
                add_bias(i, jj)
            turn_m(i)
            quant_m(i)
        sort_m(HEAD_TILES, 0)
        sort_m(HEAD_TILES, 1)
        prep_w1(2)
        for j in range(4):
            for i in range(HEAD_TILES):
                proj(i, j)
            for part in (2 * j + 3, 2 * j + 4):
                if part < 8:
                    prep_w1(part)
        nc.sync.dma_start(
            out=wraw.rearrange("p (g t) -> p g t", g=4), in_=norm2_w.rearrange("(g p t) -> p g t", g=4, p=P, t=4)
        )
        nc.sync.dma_start(
            out=braw.rearrange("p (g t) -> p g t", g=4), in_=norm2_b.rearrange("(g p t) -> p g t", g=4, p=P, t=4)
        )
        nc.vector.tensor_copy(out=wcol[:], in_=wraw[:])
        nc.vector.tensor_copy(out=bcol[:], in_=braw[:])
        for q in range(4):
            load_stage(1, q)
        step(-1, (0, 1, 2))
        step(0, (3, 4, 5))
        step(1, (6, 7))
        for s in range(2, NT + 2 + LAG):
            step(s, ())
